import numpy as np
import ml_dtypes


def mxq(x, axis, fmt="e4m3"):
    dtype, down = {"e4m3": (ml_dtypes.float8_e4m3fn, 7), "e5m2": (ml_dtypes.float8_e5m2, 14)}[fmt]
    v = np.moveaxis(np.asarray(x, np.float32).astype(ml_dtypes.bfloat16).astype(np.float64), axis, -1)
    blocks = v.reshape(v.shape[:-1] + (-1, 32))
    amax = np.abs(blocks).max(-1, keepdims=True)
    byte = np.maximum(np.where(amax > 0, np.frexp(amax)[1] - 1 + 127, 0) - down, 1)
    scale = np.exp2(byte - 127.0)
    codes = (blocks / scale).astype(np.float32).astype(dtype).astype(np.float64)
    return np.moveaxis((codes * scale).reshape(v.shape), -1, axis)


WIDE = False


def mx_kscale(k):
    if not WIDE:
        return np.ones(k)
    levels = np.array([10, -10, 5, -5, 0])
    a = np.random.permutation(np.resize(levels, k // 512 * 4)).reshape(k // 512, 4)
    idx = np.arange(k)
    return np.exp2(a[idx // 512, idx % 128 // 32])


BF16 = ml_dtypes.bfloat16


def bf(x):
    return np.asarray(x, np.float32).astype(BF16)


def f64(x):
    return np.asarray(x).astype(np.float64)


B, N, D, L = 2, 4096, 512, 256
SEGS = N // L


def setup_inputs():
    s = mx_kscale(D)
    col = np.concatenate([np.full(D, np.sqrt(SEGS)), np.ones(D)])
    return {"x": bf(np.random.standard_normal((B, N, D)) * s),
            "w_kv": bf(np.random.standard_normal((D, D + D)) * col / np.sqrt(D) / s[:, None])}


def reference(x, w_kv):
    kv = mxq(f64(x), 2, "e4m3") @ mxq(f64(w_kv), 0, "e4m3")
    k, v = kv[..., :D], kv[..., D:]
    keys_lm = k.reshape(B, L, SEGS, D).mean(axis=2)
    vals_lm = v.reshape(B, L, SEGS, D).mean(axis=2)
    return v, keys_lm, vals_lm

@@ -1,0 +1,180 @@
+from contextlib import ExitStack
+
+import concourse.mybir as mybir
+from concourse.masks import make_identity
+
+F32 = mybir.dt.float32
+BF16 = mybir.dt.bfloat16
+U32 = mybir.dt.uint32
+U8 = mybir.dt.uint8
+FP8X4 = mybir.dt.float8_e4m3fn_x4
+
+P = 128
+PACK = 4
+D = 512
+WORDS = D // 2
+TOKENS = 2 * 4096
+SEG = 16
+GROUPS = TOKENS // (P * SEG)
+ROUND = 4
+ROUNDS_PER_GROUP = SEG // ROUND
+ROUNDS = GROUPS * ROUNDS_PER_GROUP
+KEYS = 0
+VALUES = 1
+
+FLOPS = 2 * TOKENS * D * 2 * D
+
+
+def tile_ammattention_pa_t_kernel(tc, x, w_kv, out_0, out_1, out_2):
+    nc = tc.nc
+    HALVES = (slice(0, ROUND * D // 2), slice(ROUND * D // 2, ROUND * D))
+
+    x_groups = x.flatten_outer_dims().rearrange("(g s j) k -> g s (j k)", s=P, j=SEG)
+    v_groups = out_0.flatten_outer_dims().rearrange("(g s j) d -> g s (j d)", s=P, j=SEG)
+    keys_mean_groups = out_1.flatten_outer_dims().rearrange("(g s) d -> g s d", s=P)
+    vals_mean_groups = out_2.flatten_outer_dims().rearrange("(g s) d -> g s d", s=P)
+
+    with ExitStack() as ctx:
+        const = ctx.enter_context(tc.tile_pool(name="const", bufs=1))
+        x_pool = ctx.enter_context(tc.tile_pool(name="x", bufs=ROUNDS))
+        mx_pool = ctx.enter_context(tc.tile_pool(name="mx", bufs=3))
+        v_pool = ctx.enter_context(tc.tile_pool(name="v", bufs=5))
+        sum_pool = ctx.enter_context(tc.tile_pool(name="sum", bufs=2))
+        xt_banks = ctx.enter_context(tc.psum_pool(name="xt", bufs=4))
+        v_banks = ctx.enter_context(tc.psum_pool(name="vb", bufs=3))
+        keys_banks = ctx.enter_context(tc.psum_pool(name="kb", bufs=1))
+        ctx.enter_context(tc.manual_schedule())
+
+        x_tiles = []
+
+        def load_x(r):
+            g, first = divmod(r, ROUNDS_PER_GROUP)
+            x_tile = x_pool.tile([P, ROUND * D], BF16)
+            nc.sync.dma_start(
+                out=x_tile[:], in_=x_groups[g, :, first * ROUND * D : (first + 1) * ROUND * D]
+            )
+            x_tiles.append(x_tile)
+
+        load_x(0)
+        w_rows = const.tile([P, PACK, 2 * D], BF16)
+        for u in range(2):
+            nc.sync.dma_start(
+                out=w_rows[:, 2 * u : 2 * u + 2, :],
+                in_=w_kv[2 * P * u : 2 * P * (u + 1), :].rearrange("(p e) c -> p e c", e=2),
+            )
+        for r in range(1, ROUNDS):
+            load_x(r)
+
+        ident = const.tile([P, P], F32)
+        make_identity(nc, ident[:])
+
+        def transpose_round(r):
+            words = x_tiles[r][:].bitcast(F32)
+            grouped = mx_pool.tile([P, ROUND * P * PACK], BF16, align_bytes=64)
+            grouped_words = grouped[:].bitcast(F32).rearrange("p (j s u) -> p j s u", j=ROUND, u=2)
+            for pair in range(ROUND // 2):
+                xt = xt_banks.tile([P, 2, 2, P], F32)
+                for jj in range(2):
+                    for u in range(2):
+                        first = (2 * pair + jj) * WORDS + u * P
+                        nc.tensor.transpose(xt[:, jj, u, :], words[:, first : first + P], ident[:])
+                nc.scalar.copy(
+                    out=grouped_words[:, 2 * pair : 2 * pair + 2],
+                    in_=xt[:].rearrange("p j u s -> p j s u"),
+                )
+            return grouped
+
+        def quantise_round(grouped):
+            codes = mx_pool.tile([P, ROUND * P], U32, align_bytes=64)
+            scales = mx_pool.tile([P, ROUND * P], U8, align_bytes=64)
+            nc.vector.quantize_mx(out=codes[:].bitcast(FP8X4), scales=scales[:], in_=grouped[:])
+            return codes, scales
+
+        grouped = transpose_round(0)
+
+        w_grouped = const.tile([P, 2, D, PACK], BF16, align_bytes=64)
+        w_codes = const.tile([P, 2, D], U32, align_bytes=64)
+        w_scales = const.tile([P, 2, D], U8, align_bytes=64)
+        nc.vector.tensor_copy(
+            out=w_grouped[:, KEYS].rearrange("p (c i) t -> p c t i", i=4),
+            in_=w_rows[:, :, 0:D].rearrange("p t (c i) -> p c t i", i=4),
+        )
+        nc.scalar.copy(
+            out=w_grouped[:, VALUES].rearrange("p (c i) t -> p c t i", i=4),
+            in_=w_rows[:, :, D : 2 * D].rearrange("p t (c i) -> p c t i", i=4),
+        )
+        quantised = quantise_round(grouped)
+        for half in (KEYS, VALUES):
+            nc.vector.quantize_mx(
+                out=w_codes[:, half].bitcast(FP8X4),
+                scales=w_scales[:, half],
+                in_=w_grouped[:, half].rearrange("p c t -> p (c t)"),
+            )
+
+        keys_sum = None
+        vals_sum = None
+        first_rows = None
+        for r in range(ROUNDS):
+            g, in_group = divmod(r, ROUNDS_PER_GROUP)
+            codes, scales = quantised
+            if r + 1 < ROUNDS:
+                quantised = quantise_round(transpose_round(r + 1))
+
+            if in_group == 0:
+                keys_sum = keys_banks.tile([P, D], F32)
+            v_rows = v_pool.tile([P, ROUND * D], F32)
+            for jj in range(ROUND):
+                j = in_group * ROUND + jj
+                segs = slice(jj * P, (jj + 1) * P)
+                nc.tensor.matmul_mx(
+                    out=keys_sum[:],
+                    lhsT=codes[:, segs].bitcast(FP8X4),
+                    lhsT_scale=scales[:, segs],
+                    rhs=w_codes[:, KEYS].bitcast(FP8X4),
+                    rhs_scale=w_scales[:, KEYS],
+                    start=(j == 0),
+                    stop=(j == SEG - 1),
+                )
+                v_bank = v_banks.tile([P, D], F32)
+                nc.tensor.matmul_mx(
+                    out=v_bank[:],
+                    lhsT=codes[:, segs].bitcast(FP8X4),
+                    lhsT_scale=scales[:, segs],
+                    rhs=w_codes[:, VALUES].bitcast(FP8X4),
+                    rhs_scale=w_scales[:, VALUES],
+                    start=True,
+                    stop=True,
+                )
+                nc.scalar.copy(out=v_rows[:, jj * D : (jj + 1) * D], in_=v_bank[:])
+            nc.sync.dma_start(
+                out=v_groups[g, :, in_group * ROUND * D : (in_group + 1) * ROUND * D], in_=v_rows[:]
+            )
+
+            if in_group == ROUNDS_PER_GROUP - 1:
+                keys_mean = sum_pool.tile([P, D], F32)
+                nc.vector.tensor_scalar_mul(out=keys_mean[:], in0=keys_sum[:], scalar1=1.0 / SEG)
+                nc.sync.dma_start(out=keys_mean_groups[g], in_=keys_mean[:])
+
+            if in_group == 0:
+                first_rows = v_rows
+            elif in_group == 1:
+                vals_sum = sum_pool.tile([P, ROUND * D], F32)
+                for half in HALVES:
+                    nc.vector.tensor_add(
+                        out=vals_sum[:, half], in0=first_rows[:, half], in1=v_rows[:, half]
+                    )
+            else:
+                for half in HALVES:
+                    nc.vector.tensor_add(
+                        out=vals_sum[:, half], in0=vals_sum[:, half], in1=v_rows[:, half]
+                    )
+
+            if in_group == ROUNDS_PER_GROUP - 1:
+                folded = sum_pool.tile([P, 2 * D], F32)
+                nc.vector.tensor_add(
+                    out=folded[:], in0=vals_sum[:, HALVES[0]], in1=vals_sum[:, HALVES[1]]
+                )
+                vals_mean = sum_pool.tile([P, D], F32)
+                nc.vector.tensor_add(out=vals_mean[:], in0=folded[:, 0:D], in1=folded[:, D : 2 * D])
+                nc.vector.tensor_scalar_mul(out=vals_mean[:], in0=vals_mean[:], scalar1=1.0 / SEG)
+                nc.sync.dma_start(out=vals_mean_groups[g], in_=vals_mean[:])

@@ -19,6 +19,7 @@ GROUPS = TOKENS // (P * SEG)
 ROUND = 4
 ROUNDS_PER_GROUP = SEG // ROUND
 ROUNDS = GROUPS * ROUNDS_PER_GROUP
+LOOKAHEAD = 2
 KEYS = 0
 VALUES = 1
 
@@ -37,7 +38,8 @@ def tile_ammattention_pa_t_kernel(tc, x, w_kv, out_0, out_1, out_2):
     with ExitStack() as ctx:
         const = ctx.enter_context(tc.tile_pool(name="const", bufs=1))
         x_pool = ctx.enter_context(tc.tile_pool(name="x", bufs=ROUNDS))
-        mx_pool = ctx.enter_context(tc.tile_pool(name="mx", bufs=3))
+        grouped_pool = ctx.enter_context(tc.tile_pool(name="grouped", bufs=3))
+        mx_pool = ctx.enter_context(tc.tile_pool(name="mx", bufs=LOOKAHEAD + 2))
         v_pool = ctx.enter_context(tc.tile_pool(name="v", bufs=5))
         sum_pool = ctx.enter_context(tc.tile_pool(name="sum", bufs=2))
         xt_banks = ctx.enter_context(tc.psum_pool(name="xt", bufs=4))
@@ -68,9 +70,9 @@ def tile_ammattention_pa_t_kernel(tc, x, w_kv, out_0, out_1, out_2):
         ident = const.tile([P, P], F32)
         make_identity(nc, ident[:])
 
-        def transpose_round(r):
+        def transpose_round(r, vector_is_free):
             words = x_tiles[r][:].bitcast(F32)
-            grouped = mx_pool.tile([P, ROUND * P * PACK], BF16, align_bytes=64)
+            grouped = grouped_pool.tile([P, ROUND * P * PACK], BF16, align_bytes=64)
             grouped_words = grouped[:].bitcast(F32).rearrange("p (j s u) -> p j s u", j=ROUND, u=2)
             for pair in range(ROUND // 2):
                 xt = xt_banks.tile([P, 2, 2, P], F32)
@@ -78,19 +80,27 @@ def tile_ammattention_pa_t_kernel(tc, x, w_kv, out_0, out_1, out_2):
                     for u in range(2):
                         first = (2 * pair + jj) * WORDS + u * P
                         nc.tensor.transpose(xt[:, jj, u, :], words[:, first : first + P], ident[:])
-                nc.scalar.copy(
-                    out=grouped_words[:, 2 * pair : 2 * pair + 2],
-                    in_=xt[:].rearrange("p j u s -> p j s u"),
-                )
+                if vector_is_free:
+                    nc.vector.tensor_copy(
+                        out=grouped_words[:, 2 * pair : 2 * pair + 2],
+                        in_=xt[:].rearrange("p j u s -> p j s u"),
+                    )
+                else:
+                    nc.scalar.copy(
+                        out=grouped_words[:, 2 * pair : 2 * pair + 2],
+                        in_=xt[:].rearrange("p j u s -> p j s u"),
+                    )
             return grouped
+
+        quantised = []
 
         def quantise_round(grouped):
             codes = mx_pool.tile([P, ROUND * P], U32, align_bytes=64)
             scales = mx_pool.tile([P, ROUND * P], U8, align_bytes=64)
             nc.vector.quantize_mx(out=codes[:].bitcast(FP8X4), scales=scales[:], in_=grouped[:])
-            return codes, scales
+            quantised.append((codes, scales))
 
-        grouped = transpose_round(0)
+        grouped = transpose_round(0, vector_is_free=False)
 
         w_grouped = const.tile([P, 2, D, PACK], BF16, align_bytes=64)
         w_codes = const.tile([P, 2, D], U32, align_bytes=64)
@@ -103,25 +113,37 @@ def tile_ammattention_pa_t_kernel(tc, x, w_kv, out_0, out_1, out_2):
             out=w_grouped[:, VALUES].rearrange("p (c i) t -> p c t i", i=4),
             in_=w_rows[:, :, D : 2 * D].rearrange("p t (c i) -> p c t i", i=4),
         )
-        quantised = quantise_round(grouped)
+        quantise_round(grouped)
         for half in (KEYS, VALUES):
             nc.vector.quantize_mx(
                 out=w_codes[:, half].bitcast(FP8X4),
                 scales=w_scales[:, half],
                 in_=w_grouped[:, half].rearrange("p c t -> p (c t)"),
             )
+        for r in range(1, LOOKAHEAD):
+            quantise_round(transpose_round(r, vector_is_free=False))
 
         keys_sum = None
-        vals_sum = None
         first_rows = None
+        vals_sum = None
+        vals_mean = None
         for r in range(ROUNDS):
             g, in_group = divmod(r, ROUNDS_PER_GROUP)
-            codes, scales = quantised
-            if r + 1 < ROUNDS:
-                quantised = quantise_round(transpose_round(r + 1))
+            last_in_group = in_group == ROUNDS_PER_GROUP - 1
+            if r + LOOKAHEAD < ROUNDS:
+                quantise_round(transpose_round(r + LOOKAHEAD, vector_is_free=(in_group == 0)))
+            codes, scales = quantised[r]
 
             if in_group == 0:
                 keys_sum = keys_banks.tile([P, D], F32)
+            if last_in_group:
+                folded = sum_pool.tile([P, 2 * D], F32)
+                nc.vector.tensor_add(
+                    out=folded[:], in0=vals_sum[:, HALVES[0]], in1=vals_sum[:, HALVES[1]]
+                )
+                vals_mean = sum_pool.tile([P, D], F32)
+                nc.vector.tensor_add(out=vals_mean[:], in0=folded[:, 0:D], in1=folded[:, D : 2 * D])
+
             v_rows = v_pool.tile([P, ROUND * D], F32)
             for jj in range(ROUND):
                 j = in_group * ROUND + jj
@@ -135,6 +157,10 @@ def tile_ammattention_pa_t_kernel(tc, x, w_kv, out_0, out_1, out_2):
                     start=(j == 0),
                     stop=(j == SEG - 1),
                 )
+                if j == SEG - 1:
+                    keys_mean = sum_pool.tile([P, D], F32)
+                    nc.vector.tensor_scalar_mul(out=keys_mean[:], in0=keys_sum[:], scalar1=1.0 / SEG)
+                    nc.sync.dma_start(out=keys_mean_groups[g], in_=keys_mean[:])
                 v_bank = v_banks.tile([P, D], F32)
                 nc.tensor.matmul_mx(
                     out=v_bank[:],
@@ -146,14 +172,15 @@ def tile_ammattention_pa_t_kernel(tc, x, w_kv, out_0, out_1, out_2):
                     stop=True,
                 )
                 nc.scalar.copy(out=v_rows[:, jj * D : (jj + 1) * D], in_=v_bank[:])
-            nc.sync.dma_start(
-                out=v_groups[g, :, in_group * ROUND * D : (in_group + 1) * ROUND * D], in_=v_rows[:]
-            )
-
-            if in_group == ROUNDS_PER_GROUP - 1:
-                keys_mean = sum_pool.tile([P, D], F32)
-                nc.vector.tensor_scalar_mul(out=keys_mean[:], in0=keys_sum[:], scalar1=1.0 / SEG)
-                nc.sync.dma_start(out=keys_mean_groups[g], in_=keys_mean[:])
+                if last_in_group:
+                    nc.vector.tensor_add(
+                        out=vals_mean[:], in0=vals_mean[:], in1=v_rows[:, jj * D : (jj + 1) * D]
+                    )
+                if jj % 2 == 1:
+                    nc.sync.dma_start(
+                        out=v_groups[g, :, (j - 1) * D : (j + 1) * D],
+                        in_=v_rows[:, (jj - 1) * D : (jj + 1) * D],
+                    )
 
             if in_group == 0:
                 first_rows = v_rows
@@ -163,18 +190,11 @@ def tile_ammattention_pa_t_kernel(tc, x, w_kv, out_0, out_1, out_2):
                     nc.vector.tensor_add(
                         out=vals_sum[:, half], in0=first_rows[:, half], in1=v_rows[:, half]
                     )
-            else:
+            elif not last_in_group:
                 for half in HALVES:
                     nc.vector.tensor_add(
                         out=vals_sum[:, half], in0=vals_sum[:, half], in1=v_rows[:, half]
                     )
-
-            if in_group == ROUNDS_PER_GROUP - 1:
-                folded = sum_pool.tile([P, 2 * D], F32)
-                nc.vector.tensor_add(
-                    out=folded[:], in0=vals_sum[:, HALVES[0]], in1=vals_sum[:, HALVES[1]]
-                )
-                vals_mean = sum_pool.tile([P, D], F32)
-                nc.vector.tensor_add(out=vals_mean[:], in0=folded[:, 0:D], in1=folded[:, D : 2 * D])
+            else:
                 nc.vector.tensor_scalar_mul(out=vals_mean[:], in0=vals_mean[:], scalar1=1.0 / SEG)
                 nc.sync.dma_start(out=vals_mean_groups[g], in_=vals_mean[:])

@@ -28,7 +28,6 @@ FLOPS = 2 * TOKENS * D * 2 * D
 
 def tile_ammattention_pa_t_kernel(tc, x, w_kv, out_0, out_1, out_2):
     nc = tc.nc
-    HALVES = (slice(0, ROUND * D // 2), slice(ROUND * D // 2, ROUND * D))
 
     x_groups = x.flatten_outer_dims().rearrange("(g s j) k -> g s (j k)", s=P, j=SEG)
     v_groups = out_0.flatten_outer_dims().rearrange("(g s j) d -> g s (j d)", s=P, j=SEG)
@@ -42,9 +41,9 @@ def tile_ammattention_pa_t_kernel(tc, x, w_kv, out_0, out_1, out_2):
         mx_pool = ctx.enter_context(tc.tile_pool(name="mx", bufs=LOOKAHEAD + 2))
         v_pool = ctx.enter_context(tc.tile_pool(name="v", bufs=5))
         sum_pool = ctx.enter_context(tc.tile_pool(name="sum", bufs=2))
-        xt_banks = ctx.enter_context(tc.psum_pool(name="xt", bufs=4))
+        xt_banks = ctx.enter_context(tc.psum_pool(name="xt", bufs=3))
         v_banks = ctx.enter_context(tc.psum_pool(name="vb", bufs=3))
-        keys_banks = ctx.enter_context(tc.psum_pool(name="kb", bufs=1))
+        keys_banks = ctx.enter_context(tc.psum_pool(name="kb", bufs=2))
         ctx.enter_context(tc.manual_schedule())
 
         x_tiles = []
@@ -70,7 +69,7 @@ def tile_ammattention_pa_t_kernel(tc, x, w_kv, out_0, out_1, out_2):
         ident = const.tile([P, P], F32)
         make_identity(nc, ident[:])
 
-        def transpose_round(r, vector_is_free):
+        def transpose_round(r):
             words = x_tiles[r][:].bitcast(F32)
             grouped = grouped_pool.tile([P, ROUND * P * PACK], BF16, align_bytes=64)
             grouped_words = grouped[:].bitcast(F32).rearrange("p (j s u) -> p j s u", j=ROUND, u=2)
@@ -80,16 +79,10 @@ def tile_ammattention_pa_t_kernel(tc, x, w_kv, out_0, out_1, out_2):
                     for u in range(2):
                         first = (2 * pair + jj) * WORDS + u * P
                         nc.tensor.transpose(xt[:, jj, u, :], words[:, first : first + P], ident[:])
-                if vector_is_free:
-                    nc.vector.tensor_copy(
-                        out=grouped_words[:, 2 * pair : 2 * pair + 2],
-                        in_=xt[:].rearrange("p j u s -> p j s u"),
-                    )
-                else:
-                    nc.scalar.copy(
-                        out=grouped_words[:, 2 * pair : 2 * pair + 2],
-                        in_=xt[:].rearrange("p j u s -> p j s u"),
-                    )
+                nc.scalar.copy(
+                    out=grouped_words[:, 2 * pair : 2 * pair + 2],
+                    in_=xt[:].rearrange("p j u s -> p j s u"),
+                )
             return grouped
 
         quantised = []
@@ -100,7 +93,7 @@ def tile_ammattention_pa_t_kernel(tc, x, w_kv, out_0, out_1, out_2):
             nc.vector.quantize_mx(out=codes[:].bitcast(FP8X4), scales=scales[:], in_=grouped[:])
             quantised.append((codes, scales))
 
-        grouped = transpose_round(0, vector_is_free=False)
+        grouped = transpose_round(0)
 
         w_grouped = const.tile([P, 2, D, PACK], BF16, align_bytes=64)
         w_codes = const.tile([P, 2, D], U32, align_bytes=64)
@@ -121,29 +114,20 @@ def tile_ammattention_pa_t_kernel(tc, x, w_kv, out_0, out_1, out_2):
                 in_=w_grouped[:, half].rearrange("p c t -> p (c t)"),
             )
         for r in range(1, LOOKAHEAD):
-            quantise_round(transpose_round(r, vector_is_free=False))
+            quantise_round(transpose_round(r))
 
         keys_sum = None
-        first_rows = None
+        first_pair = None
         vals_sum = None
-        vals_mean = None
         for r in range(ROUNDS):
             g, in_group = divmod(r, ROUNDS_PER_GROUP)
-            last_in_group = in_group == ROUNDS_PER_GROUP - 1
             if r + LOOKAHEAD < ROUNDS:
-                quantise_round(transpose_round(r + LOOKAHEAD, vector_is_free=(in_group == 0)))
+                quantise_round(transpose_round(r + LOOKAHEAD))
             codes, scales = quantised[r]
 
             if in_group == 0:
                 keys_sum = keys_banks.tile([P, D], F32)
-            if last_in_group:
-                folded = sum_pool.tile([P, 2 * D], F32)
-                nc.vector.tensor_add(
-                    out=folded[:], in0=vals_sum[:, HALVES[0]], in1=vals_sum[:, HALVES[1]]
-                )
-                vals_mean = sum_pool.tile([P, D], F32)
-                nc.vector.tensor_add(out=vals_mean[:], in0=folded[:, 0:D], in1=folded[:, D : 2 * D])
-
+                vals_sum = sum_pool.tile([P, 2 * D], F32)
             v_rows = v_pool.tile([P, ROUND * D], F32)
             for jj in range(ROUND):
                 j = in_group * ROUND + jj
@@ -172,29 +156,18 @@ def tile_ammattention_pa_t_kernel(tc, x, w_kv, out_0, out_1, out_2):
                     stop=True,
                 )
                 nc.scalar.copy(out=v_rows[:, jj * D : (jj + 1) * D], in_=v_bank[:])
-                if last_in_group:
-                    nc.vector.tensor_add(
-                        out=vals_mean[:], in0=vals_mean[:], in1=v_rows[:, jj * D : (jj + 1) * D]
-                    )
                 if jj % 2 == 1:
-                    nc.sync.dma_start(
-                        out=v_groups[g, :, (j - 1) * D : (j + 1) * D],
-                        in_=v_rows[:, (jj - 1) * D : (jj + 1) * D],
-                    )
+                    pair = v_rows[:, (jj - 1) * D : (jj + 1) * D]
+                    nc.sync.dma_start(out=v_groups[g, :, (j - 1) * D : (j + 1) * D], in_=pair)
+                    if j == 1:
+                        first_pair = pair
+                    elif j == 3:
+                        nc.vector.tensor_add(out=vals_sum[:], in0=first_pair, in1=pair)
+                    else:
+                        nc.vector.tensor_add(out=vals_sum[:], in0=vals_sum[:], in1=pair)
 
-            if in_group == 0:
-                first_rows = v_rows
-            elif in_group == 1:
-                vals_sum = sum_pool.tile([P, ROUND * D], F32)
-                for half in HALVES:
-                    nc.vector.tensor_add(
-                        out=vals_sum[:, half], in0=first_rows[:, half], in1=v_rows[:, half]
-                    )
-            elif not last_in_group:
-                for half in HALVES:
-                    nc.vector.tensor_add(
-                        out=vals_sum[:, half], in0=vals_sum[:, half], in1=v_rows[:, half]
-                    )
-            else:
+            if in_group == ROUNDS_PER_GROUP - 1:
+                vals_mean = sum_pool.tile([P, D], F32)
+                nc.vector.tensor_add(out=vals_mean[:], in0=vals_sum[:, 0:D], in1=vals_sum[:, D : 2 * D])
                 nc.vector.tensor_scalar_mul(out=vals_mean[:], in0=vals_mean[:], scalar1=1.0 / SEG)
                 nc.sync.dma_start(out=vals_mean_groups[g], in_=vals_mean[:])

@@ -41,8 +41,9 @@ def tile_ammattention_pa_t_kernel(tc, x, w_kv, out_0, out_1, out_2):
         mx_pool = ctx.enter_context(tc.tile_pool(name="mx", bufs=LOOKAHEAD + 2))
         v_pool = ctx.enter_context(tc.tile_pool(name="v", bufs=5))
         sum_pool = ctx.enter_context(tc.tile_pool(name="sum", bufs=2))
-        xt_banks = ctx.enter_context(tc.psum_pool(name="xt", bufs=3))
+        xt_banks = ctx.enter_context(tc.psum_pool(name="xt", bufs=2))
         v_banks = ctx.enter_context(tc.psum_pool(name="vb", bufs=3))
+        tail_banks = ctx.enter_context(tc.psum_pool(name="tb", bufs=1))
         keys_banks = ctx.enter_context(tc.psum_pool(name="kb", bufs=2))
         ctx.enter_context(tc.manual_schedule())
 
@@ -119,8 +120,11 @@ def tile_ammattention_pa_t_kernel(tc, x, w_kv, out_0, out_1, out_2):
         keys_sum = None
         first_pair = None
         vals_sum = None
+        vals_head = None
+        vals_tail = None
         for r in range(ROUNDS):
             g, in_group = divmod(r, ROUNDS_PER_GROUP)
+            last_in_group = in_group == ROUNDS_PER_GROUP - 1
             if r + LOOKAHEAD < ROUNDS:
                 quantise_round(transpose_round(r + LOOKAHEAD))
             codes, scales = quantised[r]
@@ -128,6 +132,10 @@ def tile_ammattention_pa_t_kernel(tc, x, w_kv, out_0, out_1, out_2):
             if in_group == 0:
                 keys_sum = keys_banks.tile([P, D], F32)
                 vals_sum = sum_pool.tile([P, 2 * D], F32)
+            if last_in_group:
+                vals_tail = tail_banks.tile([P, D], F32)
+                vals_head = sum_pool.tile([P, D], F32)
+                nc.vector.tensor_add(out=vals_head[:], in0=vals_sum[:, 0:D], in1=vals_sum[:, D : 2 * D])
             v_rows = v_pool.tile([P, ROUND * D], F32)
             for jj in range(ROUND):
                 j = in_group * ROUND + jj
@@ -155,6 +163,16 @@ def tile_ammattention_pa_t_kernel(tc, x, w_kv, out_0, out_1, out_2):
                     start=True,
                     stop=True,
                 )
+                if last_in_group:
+                    nc.tensor.matmul_mx(
+                        out=vals_tail[:],
+                        lhsT=codes[:, segs].bitcast(FP8X4),
+                        lhsT_scale=scales[:, segs],
+                        rhs=w_codes[:, VALUES].bitcast(FP8X4),
+                        rhs_scale=w_scales[:, VALUES],
+                        start=(jj == 0),
+                        stop=(jj == ROUND - 1),
+                    )
                 nc.scalar.copy(out=v_rows[:, jj * D : (jj + 1) * D], in_=v_bank[:])
                 if jj % 2 == 1:
                     pair = v_rows[:, (jj - 1) * D : (jj + 1) * D]
@@ -163,11 +181,11 @@ def tile_ammattention_pa_t_kernel(tc, x, w_kv, out_0, out_1, out_2):
                         first_pair = pair
                     elif j == 3:
                         nc.vector.tensor_add(out=vals_sum[:], in0=first_pair, in1=pair)
-                    else:
+                    elif not last_in_group:
                         nc.vector.tensor_add(out=vals_sum[:], in0=vals_sum[:], in1=pair)
 
-            if in_group == ROUNDS_PER_GROUP - 1:
+            if last_in_group:
                 vals_mean = sum_pool.tile([P, D], F32)
-                nc.vector.tensor_add(out=vals_mean[:], in0=vals_sum[:, 0:D], in1=vals_sum[:, D : 2 * D])
+                nc.vector.tensor_add(out=vals_mean[:], in0=vals_tail[:], in1=vals_head[:])
                 nc.vector.tensor_scalar_mul(out=vals_mean[:], in0=vals_mean[:], scalar1=1.0 / SEG)
                 nc.sync.dma_start(out=vals_mean_groups[g], in_=vals_mean[:])

@@ -36,49 +36,47 @@ def tile_ammattention_pa_t_kernel(tc, x, w_kv, out_0, out_1, out_2):
 
     with ExitStack() as ctx:
         const = ctx.enter_context(tc.tile_pool(name="const", bufs=1))
-        x_pool = ctx.enter_context(tc.tile_pool(name="x", bufs=ROUNDS))
+        x_pool = ctx.enter_context(tc.tile_pool(name="x", bufs=GROUPS))
         grouped_pool = ctx.enter_context(tc.tile_pool(name="grouped", bufs=3))
         mx_pool = ctx.enter_context(tc.tile_pool(name="mx", bufs=LOOKAHEAD + 2))
         v_pool = ctx.enter_context(tc.tile_pool(name="v", bufs=5))
         sum_pool = ctx.enter_context(tc.tile_pool(name="sum", bufs=2))
-        xt_banks = ctx.enter_context(tc.psum_pool(name="xt", bufs=2))
+        xt_banks = ctx.enter_context(tc.psum_pool(name="xt", bufs=3))
         v_banks = ctx.enter_context(tc.psum_pool(name="vb", bufs=3))
-        tail_banks = ctx.enter_context(tc.psum_pool(name="tb", bufs=1))
         keys_banks = ctx.enter_context(tc.psum_pool(name="kb", bufs=2))
         ctx.enter_context(tc.manual_schedule())
 
-        x_tiles = []
+        x_tiles = [x_pool.tile([P, SEG * D], BF16, name="x_tile") for g in range(GROUPS)]
 
-        def load_x(r):
-            g, first = divmod(r, ROUNDS_PER_GROUP)
-            x_tile = x_pool.tile([P, ROUND * D], BF16)
-            nc.sync.dma_start(
-                out=x_tile[:], in_=x_groups[g, :, first * ROUND * D : (first + 1) * ROUND * D]
-            )
-            x_tiles.append(x_tile)
+        def load_x(g, first_round, rounds):
+            cols = slice(first_round * ROUND * D, (first_round + rounds) * ROUND * D)
+            nc.sync.dma_start(out=x_tiles[g][:, cols], in_=x_groups[g, :, cols])
 
-        load_x(0)
+        load_x(0, 0, 1)
         w_rows = const.tile([P, PACK, 2 * D], BF16)
         for u in range(2):
             nc.sync.dma_start(
                 out=w_rows[:, 2 * u : 2 * u + 2, :],
                 in_=w_kv[2 * P * u : 2 * P * (u + 1), :].rearrange("(p e) c -> p e c", e=2),
             )
-        for r in range(1, ROUNDS):
-            load_x(r)
+        for r in range(1, ROUNDS_PER_GROUP):
+            load_x(0, r, 1)
+        for g in range(1, GROUPS):
+            load_x(g, 0, ROUNDS_PER_GROUP)
 
         ident = const.tile([P, P], F32)
         make_identity(nc, ident[:])
 
         def transpose_round(r):
-            words = x_tiles[r][:].bitcast(F32)
+            g, in_group = divmod(r, ROUNDS_PER_GROUP)
+            words = x_tiles[g][:].bitcast(F32)
             grouped = grouped_pool.tile([P, ROUND * P * PACK], BF16, align_bytes=64)
             grouped_words = grouped[:].bitcast(F32).rearrange("p (j s u) -> p j s u", j=ROUND, u=2)
             for pair in range(ROUND // 2):
                 xt = xt_banks.tile([P, 2, 2, P], F32)
                 for jj in range(2):
                     for u in range(2):
-                        first = (2 * pair + jj) * WORDS + u * P
+                        first = (in_group * ROUND + 2 * pair + jj) * WORDS + u * P
                         nc.tensor.transpose(xt[:, jj, u, :], words[:, first : first + P], ident[:])
                 nc.scalar.copy(
                     out=grouped_words[:, 2 * pair : 2 * pair + 2],
@@ -120,11 +118,8 @@ def tile_ammattention_pa_t_kernel(tc, x, w_kv, out_0, out_1, out_2):
         keys_sum = None
         first_pair = None
         vals_sum = None
-        vals_head = None
-        vals_tail = None
         for r in range(ROUNDS):
             g, in_group = divmod(r, ROUNDS_PER_GROUP)
-            last_in_group = in_group == ROUNDS_PER_GROUP - 1
             if r + LOOKAHEAD < ROUNDS:
                 quantise_round(transpose_round(r + LOOKAHEAD))
             codes, scales = quantised[r]
@@ -132,10 +127,6 @@ def tile_ammattention_pa_t_kernel(tc, x, w_kv, out_0, out_1, out_2):
             if in_group == 0:
                 keys_sum = keys_banks.tile([P, D], F32)
                 vals_sum = sum_pool.tile([P, 2 * D], F32)
-            if last_in_group:
-                vals_tail = tail_banks.tile([P, D], F32)
-                vals_head = sum_pool.tile([P, D], F32)
-                nc.vector.tensor_add(out=vals_head[:], in0=vals_sum[:, 0:D], in1=vals_sum[:, D : 2 * D])
             v_rows = v_pool.tile([P, ROUND * D], F32)
             for jj in range(ROUND):
                 j = in_group * ROUND + jj
@@ -163,16 +154,6 @@ def tile_ammattention_pa_t_kernel(tc, x, w_kv, out_0, out_1, out_2):
                     start=True,
                     stop=True,
                 )
-                if last_in_group:
-                    nc.tensor.matmul_mx(
-                        out=vals_tail[:],
-                        lhsT=codes[:, segs].bitcast(FP8X4),
-                        lhsT_scale=scales[:, segs],
-                        rhs=w_codes[:, VALUES].bitcast(FP8X4),
-                        rhs_scale=w_scales[:, VALUES],
-                        start=(jj == 0),
-                        stop=(jj == ROUND - 1),
-                    )
                 nc.scalar.copy(out=v_rows[:, jj * D : (jj + 1) * D], in_=v_bank[:])
                 if jj % 2 == 1:
                     pair = v_rows[:, (jj - 1) * D : (jj + 1) * D]
@@ -181,11 +162,11 @@ def tile_ammattention_pa_t_kernel(tc, x, w_kv, out_0, out_1, out_2):
                         first_pair = pair
                     elif j == 3:
                         nc.vector.tensor_add(out=vals_sum[:], in0=first_pair, in1=pair)
-                    elif not last_in_group:
+                    else:
                         nc.vector.tensor_add(out=vals_sum[:], in0=vals_sum[:], in1=pair)
 
-            if last_in_group:
+            if in_group == ROUNDS_PER_GROUP - 1:
                 vals_mean = sum_pool.tile([P, D], F32)
-                nc.vector.tensor_add(out=vals_mean[:], in0=vals_tail[:], in1=vals_head[:])
+                nc.vector.tensor_add(out=vals_mean[:], in0=vals_sum[:, 0:D], in1=vals_sum[:, D : 2 * D])
                 nc.vector.tensor_scalar_mul(out=vals_mean[:], in0=vals_mean[:], scalar1=1.0 / SEG)
                 nc.sync.dma_start(out=vals_mean_groups[g], in_=vals_mean[:])

from contextlib import ExitStack

import concourse.mybir as mybir
from concourse.masks import make_identity

F32 = mybir.dt.float32
BF16 = mybir.dt.bfloat16
U32 = mybir.dt.uint32
U8 = mybir.dt.uint8
FP8X4 = mybir.dt.float8_e4m3fn_x4

P = 128
PACK = 4
D = 512
WORDS = D // 2
TOKENS = 2 * 4096
SEG = 16
GROUPS = TOKENS // (P * SEG)
ROUND = 4
ROUNDS_PER_GROUP = SEG // ROUND
ROUNDS = GROUPS * ROUNDS_PER_GROUP
LOOKAHEAD = 2
KEYS = 0
VALUES = 1

FLOPS = 2 * TOKENS * D * 2 * D


def tile_ammattention_pa_t_kernel(tc, x, w_kv, out_0, out_1, out_2):
    nc = tc.nc

    x_groups = x.flatten_outer_dims().rearrange("(g s j) k -> g s (j k)", s=P, j=SEG)
    v_groups = out_0.flatten_outer_dims().rearrange("(g s j) d -> g s (j d)", s=P, j=SEG)
    keys_mean_groups = out_1.flatten_outer_dims().rearrange("(g s) d -> g s d", s=P)
    vals_mean_groups = out_2.flatten_outer_dims().rearrange("(g s) d -> g s d", s=P)

    with ExitStack() as ctx:
        const = ctx.enter_context(tc.tile_pool(name="const", bufs=1))
        x_pool = ctx.enter_context(tc.tile_pool(name="x", bufs=GROUPS))
        grouped_pool = ctx.enter_context(tc.tile_pool(name="grouped", bufs=3))
        mx_pool = ctx.enter_context(tc.tile_pool(name="mx", bufs=LOOKAHEAD + 2))
        v_pool = ctx.enter_context(tc.tile_pool(name="v", bufs=5))
        sum_pool = ctx.enter_context(tc.tile_pool(name="sum", bufs=2))
        xt_banks = ctx.enter_context(tc.psum_pool(name="xt", bufs=3))
        v_banks = ctx.enter_context(tc.psum_pool(name="vb", bufs=3))
        keys_banks = ctx.enter_context(tc.psum_pool(name="kb", bufs=2))
        ctx.enter_context(tc.manual_schedule())

        x_tiles = [x_pool.tile([P, SEG * D], BF16, name="x_tile") for g in range(GROUPS)]

        def load_x(g, first_round, rounds):
            cols = slice(first_round * ROUND * D, (first_round + rounds) * ROUND * D)
            nc.sync.dma_start(out=x_tiles[g][:, cols], in_=x_groups[g, :, cols])

        load_x(0, 0, 1)
        w_rows = const.tile([P, PACK, 2 * D], BF16)
        for u in range(2):
            nc.sync.dma_start(
                out=w_rows[:, 2 * u : 2 * u + 2, :],
                in_=w_kv[2 * P * u : 2 * P * (u + 1), :].rearrange("(p e) c -> p e c", e=2),
            )
        for r in range(1, ROUNDS_PER_GROUP):
            load_x(0, r, 1)
        for g in range(1, GROUPS):
            load_x(g, 0, ROUNDS_PER_GROUP)

        ident = const.tile([P, P], F32)
        make_identity(nc, ident[:])

        def transpose_round(r):
            g, in_group = divmod(r, ROUNDS_PER_GROUP)
            words = x_tiles[g][:].bitcast(F32)
            grouped = grouped_pool.tile([P, ROUND * P * PACK], BF16, align_bytes=64)
            grouped_words = grouped[:].bitcast(F32).rearrange("p (j s u) -> p j s u", j=ROUND, u=2)
            for pair in range(ROUND // 2):
                xt = xt_banks.tile([P, 2, 2, P], F32)
                for jj in range(2):
                    for u in range(2):
                        first = (in_group * ROUND + 2 * pair + jj) * WORDS + u * P
                        nc.tensor.transpose(xt[:, jj, u, :], words[:, first : first + P], ident[:])
                nc.scalar.copy(
                    out=grouped_words[:, 2 * pair : 2 * pair + 2],
                    in_=xt[:].rearrange("p j u s -> p j s u"),
                )
            return grouped

        quantised = []

        def quantise_round(grouped):
            codes = mx_pool.tile([P, ROUND * P], U32, align_bytes=64)
            scales = mx_pool.tile([P, ROUND * P], U8, align_bytes=64)
            nc.vector.quantize_mx(out=codes[:].bitcast(FP8X4), scales=scales[:], in_=grouped[:])
            quantised.append((codes, scales))

        grouped = transpose_round(0)

        w_grouped = const.tile([P, 2, D, PACK], BF16, align_bytes=64)
        w_codes = const.tile([P, 2, D], U32, align_bytes=64)
        w_scales = const.tile([P, 2, D], U8, align_bytes=64)
        nc.vector.tensor_copy(
            out=w_grouped[:, KEYS].rearrange("p (c i) t -> p c t i", i=4),
            in_=w_rows[:, :, 0:D].rearrange("p t (c i) -> p c t i", i=4),
        )
        nc.scalar.copy(
            out=w_grouped[:, VALUES].rearrange("p (c i) t -> p c t i", i=4),
            in_=w_rows[:, :, D : 2 * D].rearrange("p t (c i) -> p c t i", i=4),
        )
        quantise_round(grouped)
        for half in (KEYS, VALUES):
            nc.vector.quantize_mx(
                out=w_codes[:, half].bitcast(FP8X4),
                scales=w_scales[:, half],
                in_=w_grouped[:, half].rearrange("p c t -> p (c t)"),
            )
        for r in range(1, LOOKAHEAD):
            quantise_round(transpose_round(r))

        keys_sum = None
        first_pair = None
        vals_sum = None
        for r in range(ROUNDS):
            g, in_group = divmod(r, ROUNDS_PER_GROUP)
            if r + LOOKAHEAD < ROUNDS:
                quantise_round(transpose_round(r + LOOKAHEAD))
            codes, scales = quantised[r]

            if in_group == 0:
                keys_sum = keys_banks.tile([P, D], F32)
                vals_sum = sum_pool.tile([P, 2 * D], F32)
            v_rows = v_pool.tile([P, ROUND * D], F32)
            for jj in range(ROUND):
                j = in_group * ROUND + jj
                segs = slice(jj * P, (jj + 1) * P)
                nc.tensor.matmul_mx(
                    out=keys_sum[:],
                    lhsT=codes[:, segs].bitcast(FP8X4),
                    lhsT_scale=scales[:, segs],
                    rhs=w_codes[:, KEYS].bitcast(FP8X4),
                    rhs_scale=w_scales[:, KEYS],
                    start=(j == 0),
                    stop=(j == SEG - 1),
                )
                if j == SEG - 1:
                    keys_mean = sum_pool.tile([P, D], F32)
                    nc.vector.tensor_scalar_mul(out=keys_mean[:], in0=keys_sum[:], scalar1=1.0 / SEG)
                    nc.sync.dma_start(out=keys_mean_groups[g], in_=keys_mean[:])
                v_bank = v_banks.tile([P, D], F32)
                nc.tensor.matmul_mx(
                    out=v_bank[:],
                    lhsT=codes[:, segs].bitcast(FP8X4),
                    lhsT_scale=scales[:, segs],
                    rhs=w_codes[:, VALUES].bitcast(FP8X4),
                    rhs_scale=w_scales[:, VALUES],
                    start=True,
                    stop=True,
                )
                nc.scalar.copy(out=v_rows[:, jj * D : (jj + 1) * D], in_=v_bank[:])
                if jj % 2 == 1:
                    pair = v_rows[:, (jj - 1) * D : (jj + 1) * D]
                    nc.sync.dma_start(out=v_groups[g, :, (j - 1) * D : (j + 1) * D], in_=pair)
                    if j == 1:
                        first_pair = pair
                    elif j == 3:
                        nc.vector.tensor_add(out=vals_sum[:], in0=first_pair, in1=pair)
                    else:
                        nc.vector.tensor_add(out=vals_sum[:], in0=vals_sum[:], in1=pair)

            if in_group == ROUNDS_PER_GROUP - 1:
                vals_mean = sum_pool.tile([P, D], F32)
                nc.vector.tensor_add(out=vals_mean[:], in0=vals_sum[:, 0:D], in1=vals_sum[:, D : 2 * D])
                nc.vector.tensor_scalar_mul(out=vals_mean[:], in0=vals_mean[:], scalar1=1.0 / SEG)
                nc.sync.dma_start(out=vals_mean_groups[g], in_=vals_mean[:])
